import numpy as np
import ml_dtypes


def mxq(x, axis, fmt="e4m3"):
    dtype, down = {"e4m3": (ml_dtypes.float8_e4m3fn, 7), "e5m2": (ml_dtypes.float8_e5m2, 14)}[fmt]
    v = np.moveaxis(np.asarray(x, np.float32).astype(ml_dtypes.bfloat16).astype(np.float64), axis, -1)
    blocks = v.reshape(v.shape[:-1] + (-1, 32))
    amax = np.abs(blocks).max(-1, keepdims=True)
    byte = np.maximum(np.where(amax > 0, np.frexp(amax)[1] - 1 + 127, 0) - down, 1)
    scale = np.exp2(byte - 127.0)
    codes = (blocks / scale).astype(np.float32).astype(dtype).astype(np.float64)
    return np.moveaxis((codes * scale).reshape(v.shape), -1, axis)


BF16 = ml_dtypes.bfloat16


def bf(x):
    return np.asarray(x, np.float32).astype(BF16)


def f64(x):
    return np.asarray(x).astype(np.float64)


B, F, N = 12, 512, 128
SIGMA = 2.0
RANK = 8


def setup_inputs():
    u = np.random.standard_normal((B, F, RANK))
    v = np.random.standard_normal((B, RANK, N))
    shared = sum(u[:, :, r, None] * v[:, r, None, :] for r in range(RANK)) / np.sqrt(RANK)
    emb = 0.6 * (shared + 0.5 * np.random.standard_normal((B, F, N)))
    return {"adj_in": bf(0.1 * np.random.standard_normal((B, N, N))), "emb_in": bf(emb)}


def reference(adj_in, emb_in):
    e = f64(emb_in)
    std = np.std(e, ddof=1)
    coord = e / std
    fmap = coord.shape[1]
    sq = np.sum(coord * coord, axis=1)
    cq = mxq(coord, 1, "e4m3")
    inner = cq.transpose(0, 2, 1) @ cq
    d2 = (sq[:, :, None] + sq[:, None, :] - 2.0 * inner) / fmap
    d2 = np.maximum(d2, 0.0)
    return np.exp(-d2 / SIGMA)

@@ -1,0 +1,200 @@
+from contextlib import ExitStack
+
+import concourse.mybir as mybir
+from concourse.masks import make_identity
+
+F32 = mybir.dt.float32
+BF16 = mybir.dt.bfloat16
+U32 = mybir.dt.uint32
+U8 = mybir.dt.uint8
+FP8X4 = mybir.dt.float8_e4m3fn_x4
+ALU = mybir.AluOpType
+ACT = mybir.ActivationFunctionType
+
+B, F, N = 12, 512, 128
+P = 128
+PACK = 4
+COUNT = B * F * N
+BANK_B = 4
+GROUPS = B // BANK_B
+BANK_COLS = BANK_B * N
+
+FLOPS = 2 * B * N * N * F
+BYTES = B * F * N * 2 + B * N * N * 4
+
+
+def tile_gaussian_s_kernel(tc, adj_in, emb_in, out):
+    nc = tc.nc
+    with ExitStack() as ctx:
+        keep = ctx.enter_context(tc.tile_pool(name="keep", bufs=1))
+        banks = ctx.enter_context(tc.psum_pool(name="banks", bufs=7))
+        small = ctx.enter_context(tc.psum_pool(name="small", bufs=1))
+        ctx.enter_context(tc.manual_schedule())
+
+        ident = keep.tile([P, P], F32)
+        make_identity(nc, ident[:])
+        ones_bf16 = keep.tile([P, 2], BF16)
+        nc.vector.memset(ones_bf16[:], 1.0)
+        ones_f32 = keep.tile([P, P], F32)
+        nc.vector.memset(ones_f32[:], 1.0)
+        one = keep.tile([P, 1], F32)
+        nc.vector.memset(one[:], 1.0)
+        unread = keep.tile([P, 2], F32)
+        nc.scalar.activation(out=unread[:, 0:1], in_=one[:], func=ACT.Sqrt)
+
+        raw = keep.tile([P, B, PACK, N], BF16)
+        grouped = keep.tile([P, B, N, PACK], BF16, align_bytes=64)
+        coord = keep.tile([P, GROUPS, BANK_COLS * PACK], BF16, align_bytes=64)
+        codes = keep.tile([P, GROUPS, BANK_COLS], U32, align_bytes=64)
+        planes = keep.tile([P, GROUPS, BANK_COLS], U8, align_bytes=64)
+        squares = keep.tile([P, B, F], BF16)
+        sq_raw = keep.tile([P, B], F32)
+        pair_raw = keep.tile([P, B, N], F32)
+        arg = keep.tile([P, GROUPS, BANK_COLS], F32)
+        clamped = keep.tile([P, GROUPS, BANK_COLS], F32)
+        result = keep.tile([P, GROUPS, BANK_COLS], F32)
+        sums = small.tile([P, 4], F32)
+        col_sum = sums[:, 0:1]
+        total_sum = sums[:, 1:2]
+        total_sq = sums[:, 2:3]
+
+        def group_batches(g):
+            return slice(g * BANK_B, (g + 1) * BANK_B)
+
+        for b in range(B):
+            nc.sync.dma_start(
+                out=raw[:, b], in_=emb_in[b].rearrange("(p j) n -> p j n", j=PACK)
+            )
+
+        words = grouped[:].rearrange("p b n j -> p (b n j)").bitcast(F32)
+        words = words.rearrange("p (b n u) -> p b n u", b=B, n=N)
+        for b in range(B):
+            nc.vector.tensor_copy(
+                out=grouped[:, b].rearrange("p (c i) j -> p c j i", i=4),
+                in_=raw[:, b].rearrange("p j (c i) -> p c j i", i=4),
+            )
+            for j in range(PACK):
+                nc.tensor.matmul(
+                    out=col_sum,
+                    lhsT=raw[:, b, j, :],
+                    rhs=ones_bf16[:, 0:1],
+                    start=(b == 0 and j == 0),
+                    stop=(b == B - 1 and j == PACK - 1),
+                )
+            flipped = banks.tile([P, 2 * P], F32, tag="bank")
+            for u in range(2):
+                nc.tensor.transpose(flipped[:, u * P : (u + 1) * P], words[:, b, :, u], ident[:])
+            nc.scalar.activation(
+                out=squares[:, b, :],
+                in_=flipped[:].bitcast(BF16),
+                func=ACT.Square,
+                accum_out=sq_raw[:, b : b + 1],
+            )
+
+        col_sum_sb = keep.tile([P, 1], F32)
+        nc.vector.tensor_copy(out=col_sum_sb[:], in_=col_sum)
+        nc.tensor.matmul(out=total_sum, lhsT=ones_f32[:], rhs=col_sum_sb[:], start=True, stop=True)
+        total_sum_sb = keep.tile([P, 1], F32)
+        nc.vector.tensor_copy(out=total_sum_sb[:], in_=total_sum)
+        mean_term = keep.tile([P, 1], F32)
+        nc.vector.scalar_tensor_tensor(
+            out=mean_term[:],
+            in0=total_sum_sb[:],
+            scalar=-1.0 / (COUNT * (COUNT - 1)),
+            in1=total_sum_sb[:],
+            op0=ALU.mult,
+            op1=ALU.mult,
+        )
+
+        def pair_sums(g, rows):
+            nc.vector.tensor_tensor(
+                out=pair_raw[:, group_batches(g), :],
+                in0=rows[:].rearrange("p (b m) -> p b m", b=BANK_B),
+                in1=sq_raw[:, group_batches(g)].unsqueeze(2).to_broadcast([P, BANK_B, N]),
+                op=ALU.add,
+            )
+
+        for g in range(GROUPS):
+            for b in range(g * BANK_B, (g + 1) * BANK_B):
+                nc.tensor.matmul(
+                    out=total_sq,
+                    lhsT=ones_f32[:],
+                    rhs=sq_raw[:, b : b + 1],
+                    start=(b == 0),
+                    stop=(b == B - 1),
+                )
+            rows = banks.tile([P, BANK_COLS], F32, tag="bank")
+            for i in range(BANK_B):
+                b = g * BANK_B + i
+                nc.tensor.transpose(
+                    rows[:, i * N : (i + 1) * N], sq_raw[:, b : b + 1].to_broadcast([P, P]), ident[:]
+                )
+            if g < GROUPS - 1:
+                pair_sums(g, rows)
+
+        std = keep.tile([P, 1], F32)
+        nc.scalar.activation(
+            out=std[:], in_=total_sq, func=ACT.Sqrt, scale=1.0 / (COUNT - 1), bias=mean_term[:]
+        )
+        rstd = keep.tile([P, 1], F32)
+        nc.vector.reciprocal(out=rstd[:], in_=std[:])
+
+        def flat_group(g):
+            return grouped[:, group_batches(g)].rearrange("p b n j -> p (b n j)")
+
+        for g in range(GROUPS - 1):
+            nc.vector.tensor_scalar(
+                out=coord[:, g, :], in0=flat_group(g), scalar1=rstd[:], scalar2=None, op0=ALU.mult
+            )
+        nc.scalar.activation(
+            out=coord[:, GROUPS - 1, :], in_=flat_group(GROUPS - 1), func=ACT.Copy, scale=rstd[:]
+        )
+        nc.scalar.activation(out=unread[:, 1:2], in_=std[:], func=ACT.Exp, scale=0.0)
+        neg_half_rvar = keep.tile([P, 1], F32)
+        nc.vector.scalar_tensor_tensor(
+            out=neg_half_rvar[:], in0=rstd[:], scalar=-0.5, in1=rstd[:], op0=ALU.mult, op1=ALU.mult
+        )
+
+        def products(g):
+            nc.vector.quantize_mx(
+                out=codes[:, g, :].bitcast(FP8X4), scales=planes[:, g, :], in_=coord[:, g, :]
+            )
+            inner = banks.tile([P, BANK_COLS], F32, tag="bank")
+            for i in range(BANK_B):
+                cols = slice(i * N, (i + 1) * N)
+                nc.tensor.matmul_mx(
+                    out=inner[:, cols],
+                    lhsT=codes[:, g, cols].bitcast(FP8X4),
+                    lhsT_scale=planes[:, g, cols],
+                    rhs=codes[:, g, cols].bitcast(FP8X4),
+                    rhs_scale=planes[:, g, cols],
+                    start=True,
+                    stop=True,
+                )
+            return inner
+
+        def finish(g, inner):
+            nc.vector.scalar_tensor_tensor(
+                out=arg[:, g, :],
+                in0=pair_raw[:, group_batches(g), :].rearrange("p b m -> p (b m)"),
+                scalar=neg_half_rvar[:],
+                in1=inner[:],
+                op0=ALU.mult,
+                op1=ALU.add,
+            )
+            nc.vector.tensor_scalar_min(out=clamped[:, g, :], in0=arg[:, g, :], scalar1=0.0)
+            nc.scalar.activation(
+                out=result[:, g, :], in_=clamped[:, g, :], func=ACT.Exp, scale=1.0 / F
+            )
+            nc.sync.dma_start(
+                out=out[group_batches(g)].rearrange("b n m -> n b m"),
+                in_=result[:, g, :].rearrange("p (b m) -> p b m", b=BANK_B),
+            )
+
+        inners = [products(0)]
+        for g in range(1, GROUPS):
+            inners.append(products(g))
+            if g == GROUPS - 1:
+                pair_sums(g, rows)
+            finish(g - 1, inners[g - 1])
+        finish(GROUPS - 1, inners[GROUPS - 1])

@@ -18,6 +18,8 @@ COUNT = B * F * N
 BANK_B = 4
 GROUPS = B // BANK_B
 BANK_COLS = BANK_B * N
+VECTOR_B = 2
+PAD = 8
 
 FLOPS = 2 * B * N * N * F
 BYTES = B * F * N * 2 + B * N * N * 4
@@ -40,15 +42,16 @@ def tile_gaussian_s_kernel(tc, adj_in, emb_in, out):
         one = keep.tile([P, 1], F32)
         nc.vector.memset(one[:], 1.0)
         unread = keep.tile([P, 2], F32)
-        nc.scalar.activation(out=unread[:, 0:1], in_=one[:], func=ACT.Sqrt)
+        nc.scalar.activation(out=unread[:, 0:1], in_=one[:], func=ACT.Abs_reciprocal_sqrt)
 
         raw = keep.tile([P, B, PACK, N], BF16)
         grouped = keep.tile([P, B, N, PACK], BF16, align_bytes=64)
         coord = keep.tile([P, GROUPS, BANK_COLS * PACK], BF16, align_bytes=64)
         codes = keep.tile([P, GROUPS, BANK_COLS], U32, align_bytes=64)
         planes = keep.tile([P, GROUPS, BANK_COLS], U8, align_bytes=64)
-        squares = keep.tile([P, B, F], BF16)
-        sq_raw = keep.tile([P, B], F32)
+        squares = keep.tile([P, B, F], F32)
+        flipped_sb = keep.tile([P, VECTOR_B, F], BF16)
+        sq_raw = keep.tile([P, B, PAD], F32)
         pair_raw = keep.tile([P, B, N], F32)
         arg = keep.tile([P, GROUPS, BANK_COLS], F32)
         clamped = keep.tile([P, GROUPS, BANK_COLS], F32)
@@ -68,6 +71,7 @@ def tile_gaussian_s_kernel(tc, adj_in, emb_in, out):
 
         words = grouped[:].rearrange("p b n j -> p (b n j)").bitcast(F32)
         words = words.rearrange("p (b n u) -> p b n u", b=B, n=N)
+        late = []
         for b in range(B):
             nc.vector.tensor_copy(
                 out=grouped[:, b].rearrange("p (c i) j -> p c j i", i=4),
@@ -84,12 +88,15 @@ def tile_gaussian_s_kernel(tc, adj_in, emb_in, out):
             flipped = banks.tile([P, 2 * P], F32, tag="bank")
             for u in range(2):
                 nc.tensor.transpose(flipped[:, u * P : (u + 1) * P], words[:, b, :, u], ident[:])
-            nc.scalar.activation(
-                out=squares[:, b, :],
-                in_=flipped[:].bitcast(BF16),
-                func=ACT.Square,
-                accum_out=sq_raw[:, b : b + 1],
-            )
+            if b < B - VECTOR_B:
+                nc.scalar.activation(
+                    out=squares[:, b, :],
+                    in_=flipped[:].bitcast(BF16),
+                    func=ACT.Square,
+                    accum_out=sq_raw[:, b, 0:1],
+                )
+            else:
+                late.append(flipped)
 
         col_sum_sb = keep.tile([P, 1], F32)
         nc.vector.tensor_copy(out=col_sum_sb[:], in_=col_sum)
@@ -106,11 +113,24 @@ def tile_gaussian_s_kernel(tc, adj_in, emb_in, out):
             op1=ALU.mult,
         )
 
+        for i in range(VECTOR_B):
+            b = B - VECTOR_B + i
+            nc.vector.tensor_copy(out=flipped_sb[:, i, :], in_=late[i][:].bitcast(BF16))
+            nc.vector.scalar_tensor_tensor(
+                out=squares[:, b, :],
+                in0=flipped_sb[:, i, :],
+                scalar=1.0,
+                in1=flipped_sb[:, i, :],
+                op0=ALU.mult,
+                op1=ALU.mult,
+                accum_out=sq_raw[:, b, 0:1],
+            )
+
         def pair_sums(g, rows):
             nc.vector.tensor_tensor(
                 out=pair_raw[:, group_batches(g), :],
                 in0=rows[:].rearrange("p (b m) -> p b m", b=BANK_B),
-                in1=sq_raw[:, group_batches(g)].unsqueeze(2).to_broadcast([P, BANK_B, N]),
+                in1=sq_raw[:, group_batches(g), 0:1].to_broadcast([P, BANK_B, N]),
                 op=ALU.add,
             )
 
@@ -119,7 +139,7 @@ def tile_gaussian_s_kernel(tc, adj_in, emb_in, out):
                 nc.tensor.matmul(
                     out=total_sq,
                     lhsT=ones_f32[:],
-                    rhs=sq_raw[:, b : b + 1],
+                    rhs=sq_raw[:, b, 0:1],
                     start=(b == 0),
                     stop=(b == B - 1),
                 )
@@ -127,17 +147,19 @@ def tile_gaussian_s_kernel(tc, adj_in, emb_in, out):
             for i in range(BANK_B):
                 b = g * BANK_B + i
                 nc.tensor.transpose(
-                    rows[:, i * N : (i + 1) * N], sq_raw[:, b : b + 1].to_broadcast([P, P]), ident[:]
+                    rows[:, i * N : (i + 1) * N], sq_raw[:, b, 0:1].to_broadcast([P, P]), ident[:]
                 )
             if g < GROUPS - 1:
                 pair_sums(g, rows)
 
-        std = keep.tile([P, 1], F32)
-        nc.scalar.activation(
-            out=std[:], in_=total_sq, func=ACT.Sqrt, scale=1.0 / (COUNT - 1), bias=mean_term[:]
-        )
         rstd = keep.tile([P, 1], F32)
-        nc.vector.reciprocal(out=rstd[:], in_=std[:])
+        nc.scalar.activation(
+            out=rstd[:],
+            in_=total_sq,
+            func=ACT.Abs_reciprocal_sqrt,
+            scale=1.0 / (COUNT - 1),
+            bias=mean_term[:],
+        )
 
         def flat_group(g):
             return grouped[:, group_batches(g)].rearrange("p b n j -> p (b n j)")
@@ -149,7 +171,7 @@ def tile_gaussian_s_kernel(tc, adj_in, emb_in, out):
         nc.scalar.activation(
             out=coord[:, GROUPS - 1, :], in_=flat_group(GROUPS - 1), func=ACT.Copy, scale=rstd[:]
         )
-        nc.scalar.activation(out=unread[:, 1:2], in_=std[:], func=ACT.Exp, scale=0.0)
+        nc.scalar.activation(out=unread[:, 1:2], in_=one[:], func=ACT.Exp)
         neg_half_rvar = keep.tile([P, 1], F32)
         nc.vector.scalar_tensor_tensor(
             out=neg_half_rvar[:], in0=rstd[:], scalar=-0.5, in1=rstd[:], op0=ALU.mult, op1=ALU.mult

@@ -56,10 +56,10 @@ def tile_gaussian_s_kernel(tc, adj_in, emb_in, out):
         arg = keep.tile([P, GROUPS, BANK_COLS], F32)
         clamped = keep.tile([P, GROUPS, BANK_COLS], F32)
         result = keep.tile([P, GROUPS, BANK_COLS], F32)
-        sums = small.tile([P, 4], F32)
+        sums = small.tile([P, 2 + B], F32)
         col_sum = sums[:, 0:1]
         total_sum = sums[:, 1:2]
-        total_sq = sums[:, 2:3]
+        total_sq = sums[:, 2 : 2 + B]
 
         def group_batches(g):
             return slice(g * BANK_B, (g + 1) * BANK_B)
@@ -107,7 +107,7 @@ def tile_gaussian_s_kernel(tc, adj_in, emb_in, out):
         nc.vector.scalar_tensor_tensor(
             out=mean_term[:],
             in0=total_sum_sb[:],
-            scalar=-1.0 / (COUNT * (COUNT - 1)),
+            scalar=-1.0 / (B * COUNT * (COUNT - 1)),
             in1=total_sum_sb[:],
             op0=ALU.mult,
             op1=ALU.mult,
@@ -135,13 +135,9 @@ def tile_gaussian_s_kernel(tc, adj_in, emb_in, out):
             )
 
         for g in range(GROUPS):
-            for b in range(g * BANK_B, (g + 1) * BANK_B):
+            if g == GROUPS - 1:
                 nc.tensor.matmul(
-                    out=total_sq,
-                    lhsT=ones_f32[:],
-                    rhs=sq_raw[:, b, 0:1],
-                    start=(b == 0),
-                    stop=(b == B - 1),
+                    out=total_sq, lhsT=ones_f32[:], rhs=sq_raw[:, :, 0], start=True, stop=True
                 )
             rows = banks.tile([P, BANK_COLS], F32, tag="bank")
             for i in range(BANK_B):
@@ -152,14 +148,18 @@ def tile_gaussian_s_kernel(tc, adj_in, emb_in, out):
             if g < GROUPS - 1:
                 pair_sums(g, rows)
 
-        rstd = keep.tile([P, 1], F32)
+        var_terms = keep.tile([P, B], F32)
+        var = keep.tile([P, 1], F32)
         nc.scalar.activation(
-            out=rstd[:],
+            out=var_terms[:],
             in_=total_sq,
-            func=ACT.Abs_reciprocal_sqrt,
+            func=ACT.Identity,
             scale=1.0 / (COUNT - 1),
             bias=mean_term[:],
+            accum_out=var[:],
         )
+        rstd = keep.tile([P, 1], F32)
+        nc.scalar.activation(out=rstd[:], in_=var[:], func=ACT.Abs_reciprocal_sqrt)
 
         def flat_group(g):
             return grouped[:, group_batches(g)].rearrange("p b n j -> p (b n j)")

@@ -98,24 +98,11 @@ def tile_gaussian_s_kernel(tc, adj_in, emb_in, out):
             else:
                 late.append(flipped)
 
-        col_sum_sb = keep.tile([P, 1], F32)
-        nc.vector.tensor_copy(out=col_sum_sb[:], in_=col_sum)
-        nc.tensor.matmul(out=total_sum, lhsT=ones_f32[:], rhs=col_sum_sb[:], start=True, stop=True)
-        total_sum_sb = keep.tile([P, 1], F32)
-        nc.vector.tensor_copy(out=total_sum_sb[:], in_=total_sum)
-        mean_term = keep.tile([P, 1], F32)
-        nc.vector.scalar_tensor_tensor(
-            out=mean_term[:],
-            in0=total_sum_sb[:],
-            scalar=-1.0 / (B * COUNT * (COUNT - 1)),
-            in1=total_sum_sb[:],
-            op0=ALU.mult,
-            op1=ALU.mult,
-        )
-
-        for i in range(VECTOR_B):
-            b = B - VECTOR_B + i
+        def copy_out(i):
             nc.vector.tensor_copy(out=flipped_sb[:, i, :], in_=late[i][:].bitcast(BF16))
+
+        def sum_squares(i):
+            b = B - VECTOR_B + i
             nc.vector.scalar_tensor_tensor(
                 out=squares[:, b, :],
                 in0=flipped_sb[:, i, :],
@@ -125,6 +112,25 @@ def tile_gaussian_s_kernel(tc, adj_in, emb_in, out):
                 op1=ALU.mult,
                 accum_out=sq_raw[:, b, 0:1],
             )
+
+        col_sum_sb = keep.tile([P, 1], F32)
+        total_sum_sb = keep.tile([P, 1], F32)
+        mean_term = keep.tile([P, 1], F32)
+        copy_out(0)
+        nc.vector.tensor_copy(out=col_sum_sb[:], in_=col_sum)
+        nc.tensor.matmul(out=total_sum, lhsT=ones_f32[:], rhs=col_sum_sb[:], start=True, stop=True)
+        sum_squares(0)
+        copy_out(1)
+        nc.vector.tensor_copy(out=total_sum_sb[:], in_=total_sum)
+        sum_squares(1)
+        nc.vector.scalar_tensor_tensor(
+            out=mean_term[:],
+            in0=total_sum_sb[:],
+            scalar=-1.0 / (B * COUNT * (COUNT - 1)),
+            in1=total_sum_sb[:],
+            op0=ALU.mult,
+            op1=ALU.mult,
+        )
 
         def pair_sums(g, rows):
             nc.vector.tensor_tensor(
@@ -195,7 +201,7 @@ def tile_gaussian_s_kernel(tc, adj_in, emb_in, out):
                 )
             return inner
 
-        def finish(g, inner):
+        def subtract(g, inner):
             nc.vector.scalar_tensor_tensor(
                 out=arg[:, g, :],
                 in0=pair_raw[:, group_batches(g), :].rearrange("p b m -> p (b m)"),
@@ -204,6 +210,8 @@ def tile_gaussian_s_kernel(tc, adj_in, emb_in, out):
                 op0=ALU.mult,
                 op1=ALU.add,
             )
+
+        def finish(g):
             nc.vector.tensor_scalar_min(out=clamped[:, g, :], in0=arg[:, g, :], scalar1=0.0)
             nc.scalar.activation(
                 out=result[:, g, :], in_=clamped[:, g, :], func=ACT.Exp, scale=1.0 / F
@@ -213,10 +221,11 @@ def tile_gaussian_s_kernel(tc, adj_in, emb_in, out):
                 in_=result[:, g, :].rearrange("p (b m) -> p b m", b=BANK_B),
             )
 
-        inners = [products(0)]
-        for g in range(1, GROUPS):
-            inners.append(products(g))
-            if g == GROUPS - 1:
-                pair_sums(g, rows)
-            finish(g - 1, inners[g - 1])
-        finish(GROUPS - 1, inners[GROUPS - 1])
+        inners = [products(g) for g in range(GROUPS - 1)]
+        pair_sums(GROUPS - 1, rows)
+        inners.append(products(GROUPS - 1))
+        for g in range(GROUPS):
+            subtract(g, inners[g])
+            if g >= 1:
+                finish(g - 1)
+        finish(GROUPS - 1)

@@ -19,6 +19,8 @@ BANK_B = 4
 GROUPS = B // BANK_B
 BANK_COLS = BANK_B * N
 VECTOR_B = 2
+VECTOR_FIRST = B - 2 * VECTOR_B
+SINGLE_LOADS = 4
 PAD = 8
 
 FLOPS = 2 * B * N * N * F
@@ -64,9 +66,11 @@ def tile_gaussian_s_kernel(tc, adj_in, emb_in, out):
         def group_batches(g):
             return slice(g * BANK_B, (g + 1) * BANK_B)
 
-        for b in range(B):
+        load_starts = list(range(SINGLE_LOADS)) + list(range(SINGLE_LOADS, B, 2))
+        for first, after in zip(load_starts, load_starts[1:] + [B]):
             nc.sync.dma_start(
-                out=raw[:, b], in_=emb_in[b].rearrange("(p j) n -> p j n", j=PACK)
+                out=raw[:, first:after],
+                in_=emb_in[first:after].rearrange("b (p j) n -> p b j n", j=PACK),
             )
 
         words = grouped[:].rearrange("p b n j -> p (b n j)").bitcast(F32)
@@ -88,7 +92,7 @@ def tile_gaussian_s_kernel(tc, adj_in, emb_in, out):
             flipped = banks.tile([P, 2 * P], F32, tag="bank")
             for u in range(2):
                 nc.tensor.transpose(flipped[:, u * P : (u + 1) * P], words[:, b, :, u], ident[:])
-            if b < B - VECTOR_B:
+            if not VECTOR_FIRST <= b < VECTOR_FIRST + VECTOR_B:
                 nc.scalar.activation(
                     out=squares[:, b, :],
                     in_=flipped[:].bitcast(BF16),
@@ -102,7 +106,7 @@ def tile_gaussian_s_kernel(tc, adj_in, emb_in, out):
             nc.vector.tensor_copy(out=flipped_sb[:, i, :], in_=late[i][:].bitcast(BF16))
 
         def sum_squares(i):
-            b = B - VECTOR_B + i
+            b = VECTOR_FIRST + i
             nc.vector.scalar_tensor_tensor(
                 out=squares[:, b, :],
                 in0=flipped_sb[:, i, :],

@@ -18,8 +18,9 @@ COUNT = B * F * N
 BANK_B = 4
 GROUPS = B // BANK_B
 BANK_COLS = BANK_B * N
-VECTOR_B = 2
-VECTOR_FIRST = B - 2 * VECTOR_B
+BANKS = 7
+VECTOR_B = (2, 5, 8)
+VECTOR_SLICE = slice(2, 9, 3)
 SINGLE_LOADS = 4
 PAD = 8
 
@@ -31,10 +32,12 @@ def tile_gaussian_s_kernel(tc, adj_in, emb_in, out):
     nc = tc.nc
     with ExitStack() as ctx:
         keep = ctx.enter_context(tc.tile_pool(name="keep", bufs=1))
-        banks = ctx.enter_context(tc.psum_pool(name="banks", bufs=7))
+        banks = ctx.enter_context(tc.psum_pool(name="banks", bufs=BANKS))
         small = ctx.enter_context(tc.psum_pool(name="small", bufs=1))
         ctx.enter_context(tc.manual_schedule())
 
+        ident_bf16 = keep.tile([P, P], BF16)
+        make_identity(nc, ident_bf16[:])
         ident = keep.tile([P, P], F32)
         make_identity(nc, ident[:])
         ones_bf16 = keep.tile([P, 2], BF16)
@@ -47,12 +50,12 @@ def tile_gaussian_s_kernel(tc, adj_in, emb_in, out):
         nc.scalar.activation(out=unread[:, 0:1], in_=one[:], func=ACT.Abs_reciprocal_sqrt)
 
         raw = keep.tile([P, B, PACK, N], BF16)
-        grouped = keep.tile([P, B, N, PACK], BF16, align_bytes=64)
+        grouped = keep.tile([P, B - BANK_B, N, PACK], BF16, align_bytes=64)
         coord = keep.tile([P, GROUPS, BANK_COLS * PACK], BF16, align_bytes=64)
         codes = keep.tile([P, GROUPS, BANK_COLS], U32, align_bytes=64)
         planes = keep.tile([P, GROUPS, BANK_COLS], U8, align_bytes=64)
         squares = keep.tile([P, B, F], F32)
-        flipped_sb = keep.tile([P, VECTOR_B, F], BF16)
+        stats = keep.tile([P, len(VECTOR_B), 2, 3], F32)
         sq_raw = keep.tile([P, B, PAD], F32)
         pair_raw = keep.tile([P, B, N], F32)
         arg = keep.tile([P, GROUPS, BANK_COLS], F32)
@@ -73,14 +76,7 @@ def tile_gaussian_s_kernel(tc, adj_in, emb_in, out):
                 in_=emb_in[first:after].rearrange("b (p j) n -> p b j n", j=PACK),
             )
 
-        words = grouped[:].rearrange("p b n j -> p (b n j)").bitcast(F32)
-        words = words.rearrange("p (b n u) -> p b n u", b=B, n=N)
-        late = []
-        for b in range(B):
-            nc.vector.tensor_copy(
-                out=grouped[:, b].rearrange("p (c i) j -> p c j i", i=4),
-                in_=raw[:, b].rearrange("p j (c i) -> p c j i", i=4),
-            )
+        def add_up(b):
             for j in range(PACK):
                 nc.tensor.matmul(
                     out=col_sum,
@@ -89,44 +85,61 @@ def tile_gaussian_s_kernel(tc, adj_in, emb_in, out):
                     start=(b == 0 and j == 0),
                     stop=(b == B - 1 and j == PACK - 1),
                 )
-            flipped = banks.tile([P, 2 * P], F32, tag="bank")
-            for u in range(2):
-                nc.tensor.transpose(flipped[:, u * P : (u + 1) * P], words[:, b, :, u], ident[:])
-            if not VECTOR_FIRST <= b < VECTOR_FIRST + VECTOR_B:
+
+        def regroup(b):
+            nc.vector.tensor_copy(
+                out=grouped[:, b].rearrange("p (c i) j -> p c j i", i=4),
+                in_=raw[:, b].rearrange("p j (c i) -> p c j i", i=4),
+            )
+
+        flipped = {}
+        for b in range(B):
+            if b < BANKS:
+                add_up(b)
+            if b == BANKS:
+                for later in range(BANKS, B):
+                    add_up(later)
+            flipped[b] = banks.tile([P, F], BF16, tag="bank", name="flipped")
+            for j in range(PACK):
+                nc.tensor.transpose(
+                    flipped[b][:, j * P : (j + 1) * P], raw[:, b, j, :], ident_bf16[:]
+                )
+            if b not in VECTOR_B:
                 nc.scalar.activation(
                     out=squares[:, b, :],
-                    in_=flipped[:].bitcast(BF16),
+                    in_=flipped[b][:],
                     func=ACT.Square,
                     accum_out=sq_raw[:, b, 0:1],
                 )
-            else:
-                late.append(flipped)
 
-        def copy_out(i):
-            nc.vector.tensor_copy(out=flipped_sb[:, i, :], in_=late[i][:].bitcast(BF16))
-
-        def sum_squares(i):
-            b = VECTOR_FIRST + i
-            nc.vector.scalar_tensor_tensor(
-                out=squares[:, b, :],
-                in0=flipped_sb[:, i, :],
-                scalar=1.0,
-                in1=flipped_sb[:, i, :],
-                op0=ALU.mult,
-                op1=ALU.mult,
-                accum_out=sq_raw[:, b, 0:1],
-            )
+            if b in VECTOR_B:
+                nc.vector.bn_stats(
+                    out=stats[:, VECTOR_B.index(b)].rearrange("p e s -> p (e s)"),
+                    in_=flipped[b][:],
+                )
+            if b < B - BANK_B:
+                regroup(b)
 
         col_sum_sb = keep.tile([P, 1], F32)
         total_sum_sb = keep.tile([P, 1], F32)
         mean_term = keep.tile([P, 1], F32)
-        copy_out(0)
+        mean_sq = keep.tile([P, len(VECTOR_B), 2], F32)
+        half_sq = keep.tile([P, len(VECTOR_B), 2], F32)
         nc.vector.tensor_copy(out=col_sum_sb[:], in_=col_sum)
         nc.tensor.matmul(out=total_sum, lhsT=ones_f32[:], rhs=col_sum_sb[:], start=True, stop=True)
-        sum_squares(0)
-        copy_out(1)
+        nc.vector.scalar_tensor_tensor(
+            out=mean_sq[:],
+            in0=stats[:, :, :, 1],
+            scalar=F / 2.0,
+            in1=stats[:, :, :, 1],
+            op0=ALU.mult,
+            op1=ALU.mult,
+        )
+        nc.vector.tensor_tensor(out=half_sq[:], in0=mean_sq[:], in1=stats[:, :, :, 2], op=ALU.add)
         nc.vector.tensor_copy(out=total_sum_sb[:], in_=total_sum)
-        sum_squares(1)
+        nc.vector.tensor_tensor(
+            out=sq_raw[:, VECTOR_SLICE, 0], in0=half_sq[:, :, 0], in1=half_sq[:, :, 1], op=ALU.add
+        )
         nc.vector.scalar_tensor_tensor(
             out=mean_term[:],
             in0=total_sum_sb[:],
@@ -149,7 +162,7 @@ def tile_gaussian_s_kernel(tc, adj_in, emb_in, out):
                 nc.tensor.matmul(
                     out=total_sq, lhsT=ones_f32[:], rhs=sq_raw[:, :, 0], start=True, stop=True
                 )
-            rows = banks.tile([P, BANK_COLS], F32, tag="bank")
+            rows = banks.tile([P, BANK_COLS], F32, tag="bank", name="rows")
             for i in range(BANK_B):
                 b = g * BANK_B + i
                 nc.tensor.transpose(
@@ -171,15 +184,19 @@ def tile_gaussian_s_kernel(tc, adj_in, emb_in, out):
         rstd = keep.tile([P, 1], F32)
         nc.scalar.activation(out=rstd[:], in_=var[:], func=ACT.Abs_reciprocal_sqrt)
 
-        def flat_group(g):
-            return grouped[:, group_batches(g)].rearrange("p b n j -> p (b n j)")
-
         for g in range(GROUPS - 1):
             nc.vector.tensor_scalar(
-                out=coord[:, g, :], in0=flat_group(g), scalar1=rstd[:], scalar2=None, op0=ALU.mult
+                out=coord[:, g, :],
+                in0=grouped[:, group_batches(g)].rearrange("p b n j -> p (b n j)"),
+                scalar1=rstd[:],
+                scalar2=None,
+                op0=ALU.mult,
             )
         nc.scalar.activation(
-            out=coord[:, GROUPS - 1, :], in_=flat_group(GROUPS - 1), func=ACT.Copy, scale=rstd[:]
+            out=coord[:, GROUPS - 1, :].rearrange("p (b n j) -> p b n j", b=BANK_B, j=PACK),
+            in_=raw[:, group_batches(GROUPS - 1)].rearrange("p b j n -> p b n j"),
+            func=ACT.Copy,
+            scale=rstd[:],
         )
         nc.scalar.activation(out=unread[:, 1:2], in_=one[:], func=ACT.Exp)
         neg_half_rvar = keep.tile([P, 1], F32)
@@ -191,7 +208,7 @@ def tile_gaussian_s_kernel(tc, adj_in, emb_in, out):
             nc.vector.quantize_mx(
                 out=codes[:, g, :].bitcast(FP8X4), scales=planes[:, g, :], in_=coord[:, g, :]
             )
-            inner = banks.tile([P, BANK_COLS], F32, tag="bank")
+            inner = banks.tile([P, BANK_COLS], F32, tag="bank", name="inner")
             for i in range(BANK_B):
                 cols = slice(i * N, (i + 1) * N)
                 nc.tensor.matmul_mx(

@@ -19,10 +19,14 @@ BANK_B = 4
 GROUPS = B // BANK_B
 BANK_COLS = BANK_B * N
 BANKS = 7
-VECTOR_B = (2, 5, 8)
-VECTOR_SLICE = slice(2, 9, 3)
-SINGLE_LOADS = 4
-PAD = 8
+VECTOR_B = 4
+HALVES = 2 * VECTOR_B
+SCALAR_B = range(VECTOR_B, B)
+ORDER = (4, 5, 0, 6, 1, 7, 2, 8, 3, 9, 10, 11)
+GROUPED_B = B - BANK_B
+ADDED_B = (4, 5, 6)
+LOADS = ((4, 4), (5, 5), (0, 0), (6, 6), (1, 1), (7, 8), (2, 3), (9, 11))
+SUMS_AHEAD = {9: (7,), 10: (8,), 11: (9, 10, 11)}
 
 FLOPS = 2 * B * N * N * F
 BYTES = B * F * N * 2 + B * N * N * 4
@@ -36,44 +40,44 @@ def tile_gaussian_s_kernel(tc, adj_in, emb_in, out):
         small = ctx.enter_context(tc.psum_pool(name="small", bufs=1))
         ctx.enter_context(tc.manual_schedule())
 
+        ones_f32 = keep.tile([P, P], F32)
+        nc.vector.memset(ones_f32[:], 1.0)
         ident_bf16 = keep.tile([P, P], BF16)
         make_identity(nc, ident_bf16[:])
         ident = keep.tile([P, P], F32)
         make_identity(nc, ident[:])
         ones_bf16 = keep.tile([P, 2], BF16)
         nc.vector.memset(ones_bf16[:], 1.0)
-        ones_f32 = keep.tile([P, P], F32)
-        nc.vector.memset(ones_f32[:], 1.0)
         one = keep.tile([P, 1], F32)
         nc.vector.memset(one[:], 1.0)
         unread = keep.tile([P, 2], F32)
         nc.scalar.activation(out=unread[:, 0:1], in_=one[:], func=ACT.Abs_reciprocal_sqrt)
 
         raw = keep.tile([P, B, PACK, N], BF16)
-        grouped = keep.tile([P, B - BANK_B, N, PACK], BF16, align_bytes=64)
+        grouped = keep.tile([P, GROUPED_B, N, PACK], BF16, align_bytes=64)
         coord = keep.tile([P, GROUPS, BANK_COLS * PACK], BF16, align_bytes=64)
         codes = keep.tile([P, GROUPS, BANK_COLS], U32, align_bytes=64)
         planes = keep.tile([P, GROUPS, BANK_COLS], U8, align_bytes=64)
         squares = keep.tile([P, B, F], F32)
-        stats = keep.tile([P, len(VECTOR_B), 2, 3], F32)
-        sq_raw = keep.tile([P, B, PAD], F32)
+        stats = keep.tile([P, HALVES + 1, 3], F32)
+        added = keep.tile([P, len(ADDED_B)], F32)
+        sq_raw = keep.tile([P, B], F32)
         pair_raw = keep.tile([P, B, N], F32)
-        arg = keep.tile([P, GROUPS, BANK_COLS], F32)
-        clamped = keep.tile([P, GROUPS, BANK_COLS], F32)
-        result = keep.tile([P, GROUPS, BANK_COLS], F32)
-        sums = small.tile([P, 2 + B], F32)
-        col_sum = sums[:, 0:1]
-        total_sum = sums[:, 1:2]
-        total_sq = sums[:, 2 : 2 + B]
+        arg = keep.tile([P, B, N], F32)
+        clamped = keep.tile([P, B, N], F32)
+        result = keep.tile([P, B, N], F32)
+        sums = small.tile([P, HALVES + 3], F32)
+        total_means = sums[:, 0 : HALVES + 1]
+        col_sum = sums[:, HALVES + 1 : HALVES + 2]
+        total_sq = sums[:, HALVES + 2 : HALVES + 3]
 
         def group_batches(g):
             return slice(g * BANK_B, (g + 1) * BANK_B)
 
-        load_starts = list(range(SINGLE_LOADS)) + list(range(SINGLE_LOADS, B, 2))
-        for first, after in zip(load_starts, load_starts[1:] + [B]):
+        for first, last in LOADS:
             nc.sync.dma_start(
-                out=raw[:, first:after],
-                in_=emb_in[first:after].rearrange("b (p j) n -> p b j n", j=PACK),
+                out=raw[:, first : last + 1],
+                in_=emb_in[first : last + 1].rearrange("b (p j) n -> p b j n", j=PACK),
             )
 
         def add_up(b):
@@ -82,107 +86,149 @@ def tile_gaussian_s_kernel(tc, adj_in, emb_in, out):
                     out=col_sum,
                     lhsT=raw[:, b, j, :],
                     rhs=ones_bf16[:, 0:1],
-                    start=(b == 0 and j == 0),
+                    start=(b == 7 and j == 0),
                     stop=(b == B - 1 and j == PACK - 1),
                 )
 
         def regroup(b):
-            nc.vector.tensor_copy(
-                out=grouped[:, b].rearrange("p (c i) j -> p c j i", i=4),
-                in_=raw[:, b].rearrange("p j (c i) -> p c j i", i=4),
-            )
+            if b not in ADDED_B:
+                nc.gpsimd.tensor_scalar(
+                    out=grouped[:, b],
+                    in0=raw[:, b].rearrange("p j n -> p n j"),
+                    scalar1=1.0,
+                    scalar2=0.0,
+                    op0=ALU.mult,
+                    op1=ALU.add,
+                )
+            else:
+                i = ADDED_B.index(b)
+                nc.vector.tensor_scalar(
+                    out=grouped[:, b].rearrange("p (c i) j -> p c j i", i=4),
+                    in0=raw[:, b].rearrange("p j (c i) -> p c j i", i=4),
+                    scalar1=1.0,
+                    scalar2=None,
+                    op0=ALU.mult,
+                    op1=ALU.add,
+                    accum_out=added[:, i : i + 1],
+                )
 
-        flipped = {}
-        for b in range(B):
-            if b < BANKS:
-                add_up(b)
-            if b == BANKS:
-                for later in range(BANKS, B):
-                    add_up(later)
-            flipped[b] = banks.tile([P, F], BF16, tag="bank", name="flipped")
+        def flip(b):
+            flipped = banks.tile([P, F], BF16, tag="bank", name="flipped")
             for j in range(PACK):
                 nc.tensor.transpose(
-                    flipped[b][:, j * P : (j + 1) * P], raw[:, b, j, :], ident_bf16[:]
+                    flipped[:, j * P : (j + 1) * P], raw[:, b, j, :], ident_bf16[:]
                 )
-            if b not in VECTOR_B:
-                nc.scalar.activation(
-                    out=squares[:, b, :],
-                    in_=flipped[b][:],
-                    func=ACT.Square,
-                    accum_out=sq_raw[:, b, 0:1],
-                )
+            return flipped
 
-            if b in VECTOR_B:
-                nc.vector.bn_stats(
-                    out=stats[:, VECTOR_B.index(b)].rearrange("p e s -> p (e s)"),
-                    in_=flipped[b][:],
-                )
-            if b < B - BANK_B:
+        for b in ORDER:
+            if b < GROUPED_B:
                 regroup(b)
 
-        col_sum_sb = keep.tile([P, 1], F32)
-        total_sum_sb = keep.tile([P, 1], F32)
+        def repeat_rows(g):
+            rows = banks.tile([P, BANK_COLS], F32, tag="bank", name="rows")
+            for i in range(BANK_B):
+                b = g * BANK_B + i
+                nc.tensor.transpose(
+                    rows[:, i * N : (i + 1) * N], sq_raw[:, b : b + 1].to_broadcast([P, P]), ident[:]
+                )
+            return rows
+
+        rows = {}
+        for b in ORDER:
+            for summed in SUMS_AHEAD.get(b, ()):
+                add_up(summed)
+            if b == 10:
+                rows[1] = repeat_rows(1)
+            flipped = flip(b)
+            if b in SCALAR_B:
+                nc.scalar.activation(
+                    out=squares[:, b, :],
+                    in_=flipped[:],
+                    func=ACT.Square,
+                    accum_out=sq_raw[:, b : b + 1],
+                )
+            else:
+                nc.vector.bn_stats(
+                    out=stats[:, 2 * b : 2 * b + 2].rearrange("p e s -> p (e s)"), in_=flipped[:]
+                )
+
+        means = stats[:, 0:HALVES, 1]
+        mean_sq = keep.tile([P, HALVES], F32)
+        half_sq = keep.tile([P, VECTOR_B, 2], F32)
+        unread_sums = keep.tile([P, HALVES], F32)
+        total_sum = keep.tile([P, 1], F32)
+        most_sq = keep.tile([P, 1], F32)
         mean_term = keep.tile([P, 1], F32)
-        mean_sq = keep.tile([P, len(VECTOR_B), 2], F32)
-        half_sq = keep.tile([P, len(VECTOR_B), 2], F32)
-        nc.vector.tensor_copy(out=col_sum_sb[:], in_=col_sum)
-        nc.tensor.matmul(out=total_sum, lhsT=ones_f32[:], rhs=col_sum_sb[:], start=True, stop=True)
         nc.vector.scalar_tensor_tensor(
-            out=mean_sq[:],
-            in0=stats[:, :, :, 1],
-            scalar=F / 2.0,
-            in1=stats[:, :, :, 1],
-            op0=ALU.mult,
-            op1=ALU.mult,
+            out=mean_sq[:], in0=means, scalar=F / 2.0, in1=means, op0=ALU.mult, op1=ALU.mult
         )
-        nc.vector.tensor_tensor(out=half_sq[:], in0=mean_sq[:], in1=stats[:, :, :, 2], op=ALU.add)
-        nc.vector.tensor_copy(out=total_sum_sb[:], in_=total_sum)
         nc.vector.tensor_tensor(
-            out=sq_raw[:, VECTOR_SLICE, 0], in0=half_sq[:, :, 0], in1=half_sq[:, :, 1], op=ALU.add
+            out=half_sq[:].rearrange("p b e -> p (b e)"),
+            in0=mean_sq[:],
+            in1=stats[:, 0:HALVES, 2],
+            op=ALU.add,
         )
-        nc.vector.scalar_tensor_tensor(
-            out=mean_term[:],
-            in0=total_sum_sb[:],
-            scalar=-1.0 / (B * COUNT * (COUNT - 1)),
-            in1=total_sum_sb[:],
-            op0=ALU.mult,
-            op1=ALU.mult,
+        nc.vector.tensor_tensor(
+            out=sq_raw[:, 0:VECTOR_B], in0=half_sq[:, :, 0], in1=half_sq[:, :, 1], op=ALU.add
         )
 
         def pair_sums(g, rows):
             nc.vector.tensor_tensor(
                 out=pair_raw[:, group_batches(g), :],
                 in0=rows[:].rearrange("p (b m) -> p b m", b=BANK_B),
-                in1=sq_raw[:, group_batches(g), 0:1].to_broadcast([P, BANK_B, N]),
+                in1=sq_raw[:, group_batches(g)].unsqueeze(2).to_broadcast([P, BANK_B, N]),
                 op=ALU.add,
             )
 
-        for g in range(GROUPS):
-            if g == GROUPS - 1:
-                nc.tensor.matmul(
-                    out=total_sq, lhsT=ones_f32[:], rhs=sq_raw[:, :, 0], start=True, stop=True
-                )
-            rows = banks.tile([P, BANK_COLS], F32, tag="bank", name="rows")
-            for i in range(BANK_B):
-                b = g * BANK_B + i
-                nc.tensor.transpose(
-                    rows[:, i * N : (i + 1) * N], sq_raw[:, b, 0:1].to_broadcast([P, P]), ident[:]
-                )
-            if g < GROUPS - 1:
-                pair_sums(g, rows)
+        rows[0] = repeat_rows(0)
+        pair_sums(1, rows[1])
+        nc.vector.tensor_scalar(
+            out=unread_sums[:, 0 : len(ADDED_B)],
+            in0=added[:],
+            scalar1=1.0,
+            scalar2=col_sum,
+            op0=ALU.mult,
+            op1=ALU.add,
+            accum_out=stats[:, HALVES, 1:2],
+        )
+        nc.tensor.matmul(
+            out=total_means, lhsT=ones_f32[:], rhs=stats[:, :, 1], start=True, stop=True
+        )
+        nc.vector.tensor_reduce(
+            out=most_sq[:], in_=sq_raw[:, 0 : B - 1], axis=mybir.AxisListType.X, op=ALU.add
+        )
+        nc.vector.tensor_scalar(
+            out=unread_sums[:],
+            in0=total_means[:, 0:HALVES],
+            scalar1=F / 2.0,
+            scalar2=total_means[:, HALVES : HALVES + 1],
+            op0=ALU.mult,
+            op1=ALU.add,
+            accum_out=total_sum[:],
+        )
+        nc.tensor.matmul(out=total_sq, lhsT=ones_f32[:], rhs=most_sq[:], start=True, stop=False)
+        nc.tensor.matmul(
+            out=total_sq, lhsT=ones_f32[:], rhs=sq_raw[:, B - 1 : B], start=False, stop=True
+        )
+        rows[2] = repeat_rows(2)
+        nc.vector.scalar_tensor_tensor(
+            out=mean_term[:],
+            in0=total_sum[:],
+            scalar=-1.0 / (COUNT * (COUNT - 1)),
+            in1=total_sum[:],
+            op0=ALU.mult,
+            op1=ALU.mult,
+        )
+        pair_sums(0, rows[0])
 
-        var_terms = keep.tile([P, B], F32)
-        var = keep.tile([P, 1], F32)
+        rstd = keep.tile([P, 1], F32)
         nc.scalar.activation(
-            out=var_terms[:],
+            out=rstd[:],
             in_=total_sq,
-            func=ACT.Identity,
+            func=ACT.Abs_reciprocal_sqrt,
             scale=1.0 / (COUNT - 1),
             bias=mean_term[:],
-            accum_out=var[:],
         )
-        rstd = keep.tile([P, 1], F32)
-        nc.scalar.activation(out=rstd[:], in_=var[:], func=ACT.Abs_reciprocal_sqrt)
 
         for g in range(GROUPS - 1):
             nc.vector.tensor_scalar(
@@ -198,6 +244,14 @@ def tile_gaussian_s_kernel(tc, adj_in, emb_in, out):
             func=ACT.Copy,
             scale=rstd[:],
         )
+        for b in range(2 * BANK_B, B):
+            i = b - 2 * BANK_B
+            nc.scalar.activation(
+                out=pair_raw[:, b, :],
+                in_=rows[2][:, i * N : (i + 1) * N],
+                func=ACT.Identity,
+                bias=sq_raw[:, b : b + 1],
+            )
         nc.scalar.activation(out=unread[:, 1:2], in_=one[:], func=ACT.Exp)
         neg_half_rvar = keep.tile([P, 1], F32)
         nc.vector.scalar_tensor_tensor(
@@ -222,31 +276,44 @@ def tile_gaussian_s_kernel(tc, adj_in, emb_in, out):
                 )
             return inner
 
-        def subtract(g, inner):
+        def subtract(first, after, inner):
             nc.vector.scalar_tensor_tensor(
-                out=arg[:, g, :],
-                in0=pair_raw[:, group_batches(g), :].rearrange("p b m -> p (b m)"),
+                out=arg[:, first:after, :],
+                in0=pair_raw[:, first:after, :],
                 scalar=neg_half_rvar[:],
-                in1=inner[:],
+                in1=inner.rearrange("p (b m) -> p b m", m=N),
                 op0=ALU.mult,
                 op1=ALU.add,
             )
 
-        def finish(g):
-            nc.vector.tensor_scalar_min(out=clamped[:, g, :], in0=arg[:, g, :], scalar1=0.0)
-            nc.scalar.activation(
-                out=result[:, g, :], in_=clamped[:, g, :], func=ACT.Exp, scale=1.0 / F
-            )
-            nc.sync.dma_start(
-                out=out[group_batches(g)].rearrange("b n m -> n b m"),
-                in_=result[:, g, :].rearrange("p (b m) -> p b m", b=BANK_B),
+        def clamp(first, after):
+            nc.vector.tensor_scalar_min(
+                out=clamped[:, first:after, :], in0=arg[:, first:after, :], scalar1=0.0
             )
 
-        inners = [products(g) for g in range(GROUPS - 1)]
-        pair_sums(GROUPS - 1, rows)
-        inners.append(products(GROUPS - 1))
-        for g in range(GROUPS):
-            subtract(g, inners[g])
-            if g >= 1:
-                finish(g - 1)
-        finish(GROUPS - 1)
+        def finish(first, after):
+            nc.scalar.activation(
+                out=result[:, first:after, :],
+                in_=clamped[:, first:after, :],
+                func=ACT.Exp,
+                scale=1.0 / F,
+            )
+            nc.sync.dma_start(
+                out=out[first:after].rearrange("b n m -> n b m"), in_=result[:, first:after, :]
+            )
+
+        inner0 = products(0)
+        inner1 = products(1)
+        subtract(0, 4, inner0[:])
+        inner2 = products(2)
+        clamp(0, 4)
+        finish(0, 4)
+        subtract(4, 8, inner1[:])
+        subtract(8, 10, inner2[:, : 2 * N])
+        clamp(4, 8)
+        finish(4, 8)
+        subtract(10, 12, inner2[:, 2 * N :])
+        clamp(8, 10)
+        finish(8, 10)
+        clamp(10, 12)
+        finish(10, 12)

@@ -19,14 +19,16 @@ BANK_B = 4
 GROUPS = B // BANK_B
 BANK_COLS = BANK_B * N
 BANKS = 7
-VECTOR_B = 4
+VECTOR_B = 5
 HALVES = 2 * VECTOR_B
 SCALAR_B = range(VECTOR_B, B)
-ORDER = (4, 5, 0, 6, 1, 7, 2, 8, 3, 9, 10, 11)
+ORDER = (5, 6, 0, 7, 1, 8, 2, 9, 3, 10, 4, 11)
 GROUPED_B = B - BANK_B
-ADDED_B = (4, 5, 6)
-LOADS = ((4, 4), (5, 5), (0, 0), (6, 6), (1, 1), (7, 8), (2, 3), (9, 11))
-SUMS_AHEAD = {9: (7,), 10: (8,), 11: (9, 10, 11)}
+ADDED_B = (5, 6, 7)
+LOADS = ((5, 5), (6, 6), (0, 0), (7, 7), (1, 2), (8, 9), (3, 4), (10, 11))
+SUMMED_B = range(8, B)
+
+WARM_UP = 3
 
 FLOPS = 2 * B * N * N * F
 BYTES = B * F * N * 2 + B * N * N * 4
@@ -42,6 +44,11 @@ def tile_gaussian_s_kernel(tc, adj_in, emb_in, out):
 
         ones_f32 = keep.tile([P, P], F32)
         nc.vector.memset(ones_f32[:], 1.0)
+        sums = small.tile([P, HALVES + 3 + P], F32)
+        for i in range(WARM_UP):
+            nc.tensor.matmul(
+                out=sums[:, HALVES + 3 :], lhsT=ones_f32[:], rhs=ones_f32[:], start=True, stop=True
+            )
         ident_bf16 = keep.tile([P, P], BF16)
         make_identity(nc, ident_bf16[:])
         ident = keep.tile([P, P], F32)
@@ -66,7 +73,6 @@ def tile_gaussian_s_kernel(tc, adj_in, emb_in, out):
         arg = keep.tile([P, B, N], F32)
         clamped = keep.tile([P, B, N], F32)
         result = keep.tile([P, B, N], F32)
-        sums = small.tile([P, HALVES + 3], F32)
         total_means = sums[:, 0 : HALVES + 1]
         col_sum = sums[:, HALVES + 1 : HALVES + 2]
         total_sq = sums[:, HALVES + 2 : HALVES + 3]
@@ -86,8 +92,8 @@ def tile_gaussian_s_kernel(tc, adj_in, emb_in, out):
                     out=col_sum,
                     lhsT=raw[:, b, j, :],
                     rhs=ones_bf16[:, 0:1],
-                    start=(b == 7 and j == 0),
-                    stop=(b == B - 1 and j == PACK - 1),
+                    start=(b == SUMMED_B[0] and j == 0),
+                    stop=(b == SUMMED_B[-1] and j == PACK - 1),
                 )
 
         def regroup(b):
@@ -133,12 +139,10 @@ def tile_gaussian_s_kernel(tc, adj_in, emb_in, out):
                 )
             return rows
 
-        rows = {}
         for b in ORDER:
-            for summed in SUMS_AHEAD.get(b, ()):
-                add_up(summed)
-            if b == 10:
-                rows[1] = repeat_rows(1)
+            if b == ORDER[-1]:
+                for summed in SUMMED_B:
+                    add_up(summed)
             flipped = flip(b)
             if b in SCALAR_B:
                 nc.scalar.activation(
@@ -157,10 +161,19 @@ def tile_gaussian_s_kernel(tc, adj_in, emb_in, out):
         half_sq = keep.tile([P, VECTOR_B, 2], F32)
         unread_sums = keep.tile([P, HALVES], F32)
         total_sum = keep.tile([P, 1], F32)
-        most_sq = keep.tile([P, 1], F32)
+        point_sq = keep.tile([P, 1], F32)
         mean_term = keep.tile([P, 1], F32)
         nc.vector.scalar_tensor_tensor(
             out=mean_sq[:], in0=means, scalar=F / 2.0, in1=means, op0=ALU.mult, op1=ALU.mult
+        )
+        nc.vector.tensor_scalar(
+            out=unread_sums[:, 0 : len(ADDED_B)],
+            in0=added[:],
+            scalar1=1.0,
+            scalar2=col_sum,
+            op0=ALU.mult,
+            op1=ALU.add,
+            accum_out=stats[:, HALVES, 1:2],
         )
         nc.vector.tensor_tensor(
             out=half_sq[:].rearrange("p b e -> p (b e)"),
@@ -180,22 +193,12 @@ def tile_gaussian_s_kernel(tc, adj_in, emb_in, out):
                 op=ALU.add,
             )
 
-        rows[0] = repeat_rows(0)
-        pair_sums(1, rows[1])
-        nc.vector.tensor_scalar(
-            out=unread_sums[:, 0 : len(ADDED_B)],
-            in0=added[:],
-            scalar1=1.0,
-            scalar2=col_sum,
-            op0=ALU.mult,
-            op1=ALU.add,
-            accum_out=stats[:, HALVES, 1:2],
-        )
         nc.tensor.matmul(
             out=total_means, lhsT=ones_f32[:], rhs=stats[:, :, 1], start=True, stop=True
         )
+        rows = [repeat_rows(0)]
         nc.vector.tensor_reduce(
-            out=most_sq[:], in_=sq_raw[:, 0 : B - 1], axis=mybir.AxisListType.X, op=ALU.add
+            out=point_sq[:], in_=sq_raw[:], axis=mybir.AxisListType.X, op=ALU.add
         )
         nc.vector.tensor_scalar(
             out=unread_sums[:],
@@ -206,11 +209,8 @@ def tile_gaussian_s_kernel(tc, adj_in, emb_in, out):
             op1=ALU.add,
             accum_out=total_sum[:],
         )
-        nc.tensor.matmul(out=total_sq, lhsT=ones_f32[:], rhs=most_sq[:], start=True, stop=False)
-        nc.tensor.matmul(
-            out=total_sq, lhsT=ones_f32[:], rhs=sq_raw[:, B - 1 : B], start=False, stop=True
-        )
-        rows[2] = repeat_rows(2)
+        nc.tensor.matmul(out=total_sq, lhsT=ones_f32[:], rhs=point_sq[:], start=True, stop=True)
+        rows += [repeat_rows(1), repeat_rows(2)]
         nc.vector.scalar_tensor_tensor(
             out=mean_term[:],
             in0=total_sum[:],
@@ -244,11 +244,11 @@ def tile_gaussian_s_kernel(tc, adj_in, emb_in, out):
             func=ACT.Copy,
             scale=rstd[:],
         )
-        for b in range(2 * BANK_B, B):
-            i = b - 2 * BANK_B
+        for b in range(BANK_B, B):
+            i = b % BANK_B
             nc.scalar.activation(
                 out=pair_raw[:, b, :],
-                in_=rows[2][:, i * N : (i + 1) * N],
+                in_=rows[b // BANK_B][:, i * N : (i + 1) * N],
                 func=ACT.Identity,
                 bias=sq_raw[:, b : b + 1],
             )

@@ -1,3 +1,4 @@
+import math
 from contextlib import ExitStack
 
 import concourse.mybir as mybir
@@ -22,10 +23,11 @@ BANKS = 7
 VECTOR_B = 5
 HALVES = 2 * VECTOR_B
 SCALAR_B = range(VECTOR_B, B)
+SCALAR_ROWS = (len(SCALAR_B) + 1) // 2
 ORDER = (5, 6, 0, 7, 1, 8, 2, 9, 3, 10, 4, 11)
-GROUPED_B = B - BANK_B
+GROUPED_B = 10
 ADDED_B = (5, 6, 7)
-LOADS = ((5, 5), (6, 6), (0, 0), (7, 7), (1, 2), (8, 9), (3, 4), (10, 11))
+LOADS = tuple((b, b) for b in ORDER)
 SUMMED_B = range(8, B)
 
 WARM_UP = 3
@@ -44,10 +46,10 @@ def tile_gaussian_s_kernel(tc, adj_in, emb_in, out):
 
         ones_f32 = keep.tile([P, P], F32)
         nc.vector.memset(ones_f32[:], 1.0)
-        sums = small.tile([P, HALVES + 3 + P], F32)
+        sums = small.tile([P, HALVES + 2 + P], F32)
         for i in range(WARM_UP):
             nc.tensor.matmul(
-                out=sums[:, HALVES + 3 :], lhsT=ones_f32[:], rhs=ones_f32[:], start=True, stop=True
+                out=sums[:, HALVES + 2 :], lhsT=ones_f32[:], rhs=ones_f32[:], start=True, stop=True
             )
         ident_bf16 = keep.tile([P, P], BF16)
         make_identity(nc, ident_bf16[:])
@@ -62,20 +64,28 @@ def tile_gaussian_s_kernel(tc, adj_in, emb_in, out):
 
         raw = keep.tile([P, B, PACK, N], BF16)
         grouped = keep.tile([P, GROUPED_B, N, PACK], BF16, align_bytes=64)
-        coord = keep.tile([P, GROUPS, BANK_COLS * PACK], BF16, align_bytes=64)
+        coord = keep.tile([P, B, N * PACK], BF16, align_bytes=64)
         codes = keep.tile([P, GROUPS, BANK_COLS], U32, align_bytes=64)
         planes = keep.tile([P, GROUPS, BANK_COLS], U8, align_bytes=64)
         squares = keep.tile([P, B, F], F32)
-        stats = keep.tile([P, HALVES + 1, 3], F32)
+        stats = keep.tile([P, HALVES + SCALAR_ROWS, 3], F32)
+        nc.vector.memset(stats[:, HALVES:, :], 0.0)
         added = keep.tile([P, len(ADDED_B)], F32)
-        sq_raw = keep.tile([P, B], F32)
+        sq_vector = keep.tile([P, VECTOR_B], F32)
+
+        def sq_raw(b):
+            if b in SCALAR_B:
+                i = b - VECTOR_B
+                slot = 2 * (i % 2)
+                return stats[:, HALVES + i // 2, slot : slot + 1]
+            return sq_vector[:, b : b + 1]
+
         pair_raw = keep.tile([P, B, N], F32)
         arg = keep.tile([P, B, N], F32)
         clamped = keep.tile([P, B, N], F32)
         result = keep.tile([P, B, N], F32)
         total_means = sums[:, 0 : HALVES + 1]
         col_sum = sums[:, HALVES + 1 : HALVES + 2]
-        total_sq = sums[:, HALVES + 2 : HALVES + 3]
 
         def group_batches(g):
             return slice(g * BANK_B, (g + 1) * BANK_B)
@@ -126,46 +136,40 @@ def tile_gaussian_s_kernel(tc, adj_in, emb_in, out):
                 )
             return flipped
 
-        for b in ORDER:
-            if b < GROUPED_B:
-                regroup(b)
+        for b in ADDED_B + (0, 1, 2, 3, 4, 8, 9):
+            regroup(b)
 
         def repeat_rows(g):
             rows = banks.tile([P, BANK_COLS], F32, tag="bank", name="rows")
             for i in range(BANK_B):
                 b = g * BANK_B + i
                 nc.tensor.transpose(
-                    rows[:, i * N : (i + 1) * N], sq_raw[:, b : b + 1].to_broadcast([P, P]), ident[:]
+                    rows[:, i * N : (i + 1) * N], sq_raw(b).to_broadcast([P, P]), ident[:]
                 )
             return rows
 
         for b in ORDER:
-            if b == ORDER[-1]:
-                for summed in SUMMED_B:
-                    add_up(summed)
             flipped = flip(b)
             if b in SCALAR_B:
                 nc.scalar.activation(
                     out=squares[:, b, :],
                     in_=flipped[:],
                     func=ACT.Square,
-                    accum_out=sq_raw[:, b : b + 1],
+                    accum_out=sq_raw(b),
                 )
             else:
                 nc.vector.bn_stats(
                     out=stats[:, 2 * b : 2 * b + 2].rearrange("p e s -> p (e s)"), in_=flipped[:]
                 )
 
+        for b in SUMMED_B:
+            add_up(b)
+
         means = stats[:, 0:HALVES, 1]
-        mean_sq = keep.tile([P, HALVES], F32)
-        half_sq = keep.tile([P, VECTOR_B, 2], F32)
         unread_sums = keep.tile([P, HALVES], F32)
         total_sum = keep.tile([P, 1], F32)
         point_sq = keep.tile([P, 1], F32)
         mean_term = keep.tile([P, 1], F32)
-        nc.vector.scalar_tensor_tensor(
-            out=mean_sq[:], in0=means, scalar=F / 2.0, in1=means, op0=ALU.mult, op1=ALU.mult
-        )
         nc.vector.tensor_scalar(
             out=unread_sums[:, 0 : len(ADDED_B)],
             in0=added[:],
@@ -175,30 +179,22 @@ def tile_gaussian_s_kernel(tc, adj_in, emb_in, out):
             op1=ALU.add,
             accum_out=stats[:, HALVES, 1:2],
         )
-        nc.vector.tensor_tensor(
-            out=half_sq[:].rearrange("p b e -> p (b e)"),
-            in0=mean_sq[:],
-            in1=stats[:, 0:HALVES, 2],
-            op=ALU.add,
+        nc.scalar.activation(
+            out=stats[:, 0:HALVES, 0], in_=means, func=ACT.Square, scale=math.sqrt(F / 2.0)
         )
-        nc.vector.tensor_tensor(
-            out=sq_raw[:, 0:VECTOR_B], in0=half_sq[:, :, 0], in1=half_sq[:, :, 1], op=ALU.add
-        )
-
-        def pair_sums(g, rows):
-            nc.vector.tensor_tensor(
-                out=pair_raw[:, group_batches(g), :],
-                in0=rows[:].rearrange("p (b m) -> p b m", b=BANK_B),
-                in1=sq_raw[:, group_batches(g)].unsqueeze(2).to_broadcast([P, BANK_B, N]),
-                op=ALU.add,
-            )
-
         nc.tensor.matmul(
-            out=total_means, lhsT=ones_f32[:], rhs=stats[:, :, 1], start=True, stop=True
+            out=total_means, lhsT=ones_f32[:], rhs=stats[:, 0 : HALVES + 1, 1], start=True, stop=True
         )
-        rows = [repeat_rows(0)]
         nc.vector.tensor_reduce(
-            out=point_sq[:], in_=sq_raw[:], axis=mybir.AxisListType.X, op=ALU.add
+            out=point_sq[:], in_=stats[:, :, 0:3:2], axis=mybir.AxisListType.XY, op=ALU.add
+        )
+        total_sq = banks.tile([P, 1], F32, tag="bank")
+        nc.tensor.matmul(out=total_sq[:], lhsT=ones_f32[:], rhs=point_sq[:], start=True, stop=True)
+        nc.vector.tensor_reduce(
+            out=sq_vector[:],
+            in_=stats[:, 0:HALVES, 0:3:2].rearrange("p (b e) s -> p b e s", e=2),
+            axis=mybir.AxisListType.XY,
+            op=ALU.add,
         )
         nc.vector.tensor_scalar(
             out=unread_sums[:],
@@ -209,48 +205,48 @@ def tile_gaussian_s_kernel(tc, adj_in, emb_in, out):
             op1=ALU.add,
             accum_out=total_sum[:],
         )
-        nc.tensor.matmul(out=total_sq, lhsT=ones_f32[:], rhs=point_sq[:], start=True, stop=True)
-        rows += [repeat_rows(1), repeat_rows(2)]
-        nc.vector.scalar_tensor_tensor(
+
+        rows = [repeat_rows(g) for g in range(GROUPS)]
+        nc.scalar.activation(
             out=mean_term[:],
-            in0=total_sum[:],
-            scalar=-1.0 / (COUNT * (COUNT - 1)),
-            in1=total_sum[:],
-            op0=ALU.mult,
-            op1=ALU.mult,
+            in_=total_sum[:],
+            func=ACT.Square,
+            scale=1.0 / math.sqrt(COUNT * (COUNT - 1)),
         )
-        pair_sums(0, rows[0])
 
         rstd = keep.tile([P, 1], F32)
         nc.scalar.activation(
             out=rstd[:],
-            in_=total_sq,
+            in_=total_sq[:],
             func=ACT.Abs_reciprocal_sqrt,
-            scale=1.0 / (COUNT - 1),
+            scale=-1.0 / (COUNT - 1),
             bias=mean_term[:],
         )
 
-        for g in range(GROUPS - 1):
+        def scale_on_vector(first, after):
             nc.vector.tensor_scalar(
-                out=coord[:, g, :],
-                in0=grouped[:, group_batches(g)].rearrange("p b n j -> p (b n j)"),
+                out=coord[:, first:after, :],
+                in0=grouped[:, first:after].rearrange("p b n j -> p b (n j)"),
                 scalar1=rstd[:],
                 scalar2=None,
                 op0=ALU.mult,
             )
+
+        scale_on_vector(0, 4)
+        scale_on_vector(4, 8)
         nc.scalar.activation(
-            out=coord[:, GROUPS - 1, :].rearrange("p (b n j) -> p b n j", b=BANK_B, j=PACK),
-            in_=raw[:, group_batches(GROUPS - 1)].rearrange("p b j n -> p b n j"),
+            out=coord[:, GROUPED_B:].rearrange("p b (n j) -> p b n j", j=PACK),
+            in_=raw[:, GROUPED_B:].rearrange("p b j n -> p b n j"),
             func=ACT.Copy,
             scale=rstd[:],
         )
-        for b in range(BANK_B, B):
+        for b in range(B):
             i = b % BANK_B
             nc.scalar.activation(
                 out=pair_raw[:, b, :],
                 in_=rows[b // BANK_B][:, i * N : (i + 1) * N],
                 func=ACT.Identity,
-                bias=sq_raw[:, b : b + 1],
+                bias=sq_raw(b),
             )
         nc.scalar.activation(out=unread[:, 1:2], in_=one[:], func=ACT.Exp)
         neg_half_rvar = keep.tile([P, 1], F32)
@@ -260,7 +256,9 @@ def tile_gaussian_s_kernel(tc, adj_in, emb_in, out):
 
         def products(g):
             nc.vector.quantize_mx(
-                out=codes[:, g, :].bitcast(FP8X4), scales=planes[:, g, :], in_=coord[:, g, :]
+                out=codes[:, g, :].bitcast(FP8X4),
+                scales=planes[:, g, :],
+                in_=coord[:, group_batches(g)].rearrange("p b c -> p (b c)"),
             )
             inner = banks.tile([P, BANK_COLS], F32, tag="bank", name="inner")
             for i in range(BANK_B):
@@ -304,6 +302,7 @@ def tile_gaussian_s_kernel(tc, adj_in, emb_in, out):
 
         inner0 = products(0)
         inner1 = products(1)
+        scale_on_vector(8, GROUPED_B)
         subtract(0, 4, inner0[:])
         inner2 = products(2)
         clamp(0, 4)

import math
from contextlib import ExitStack

import concourse.mybir as mybir
from concourse.masks import make_identity

F32 = mybir.dt.float32
BF16 = mybir.dt.bfloat16
U32 = mybir.dt.uint32
U8 = mybir.dt.uint8
FP8X4 = mybir.dt.float8_e4m3fn_x4
ALU = mybir.AluOpType
ACT = mybir.ActivationFunctionType

B, F, N = 12, 512, 128
P = 128
PACK = 4
COUNT = B * F * N
BANK_B = 4
GROUPS = B // BANK_B
BANK_COLS = BANK_B * N
BANKS = 7
VECTOR_B = 5
HALVES = 2 * VECTOR_B
SCALAR_B = range(VECTOR_B, B)
SCALAR_ROWS = (len(SCALAR_B) + 1) // 2
ORDER = (5, 6, 0, 7, 1, 8, 2, 9, 3, 10, 4, 11)
GROUPED_B = 10
ADDED_B = (5, 6, 7)
LOADS = tuple((b, b) for b in ORDER)
SUMMED_B = range(8, B)

WARM_UP = 3

FLOPS = 2 * B * N * N * F
BYTES = B * F * N * 2 + B * N * N * 4


def tile_gaussian_s_kernel(tc, adj_in, emb_in, out):
    nc = tc.nc
    with ExitStack() as ctx:
        keep = ctx.enter_context(tc.tile_pool(name="keep", bufs=1))
        banks = ctx.enter_context(tc.psum_pool(name="banks", bufs=BANKS))
        small = ctx.enter_context(tc.psum_pool(name="small", bufs=1))
        ctx.enter_context(tc.manual_schedule())

        ones_f32 = keep.tile([P, P], F32)
        nc.vector.memset(ones_f32[:], 1.0)
        sums = small.tile([P, HALVES + 2 + P], F32)
        for i in range(WARM_UP):
            nc.tensor.matmul(
                out=sums[:, HALVES + 2 :], lhsT=ones_f32[:], rhs=ones_f32[:], start=True, stop=True
            )
        ident_bf16 = keep.tile([P, P], BF16)
        make_identity(nc, ident_bf16[:])
        ident = keep.tile([P, P], F32)
        make_identity(nc, ident[:])
        ones_bf16 = keep.tile([P, 2], BF16)
        nc.vector.memset(ones_bf16[:], 1.0)
        one = keep.tile([P, 1], F32)
        nc.vector.memset(one[:], 1.0)
        unread = keep.tile([P, 2], F32)
        nc.scalar.activation(out=unread[:, 0:1], in_=one[:], func=ACT.Abs_reciprocal_sqrt)

        raw = keep.tile([P, B, PACK, N], BF16)
        grouped = keep.tile([P, GROUPED_B, N, PACK], BF16, align_bytes=64)
        coord = keep.tile([P, B, N * PACK], BF16, align_bytes=64)
        codes = keep.tile([P, GROUPS, BANK_COLS], U32, align_bytes=64)
        planes = keep.tile([P, GROUPS, BANK_COLS], U8, align_bytes=64)
        squares = keep.tile([P, B, F], F32)
        stats = keep.tile([P, HALVES + SCALAR_ROWS, 3], F32)
        nc.vector.memset(stats[:, HALVES:, :], 0.0)
        added = keep.tile([P, len(ADDED_B)], F32)
        sq_vector = keep.tile([P, VECTOR_B], F32)

        def sq_raw(b):
            if b in SCALAR_B:
                i = b - VECTOR_B
                slot = 2 * (i % 2)
                return stats[:, HALVES + i // 2, slot : slot + 1]
            return sq_vector[:, b : b + 1]

        pair_raw = keep.tile([P, B, N], F32)
        arg = keep.tile([P, B, N], F32)
        clamped = keep.tile([P, B, N], F32)
        result = keep.tile([P, B, N], F32)
        total_means = sums[:, 0 : HALVES + 1]
        col_sum = sums[:, HALVES + 1 : HALVES + 2]

        def group_batches(g):
            return slice(g * BANK_B, (g + 1) * BANK_B)

        for first, last in LOADS:
            nc.sync.dma_start(
                out=raw[:, first : last + 1],
                in_=emb_in[first : last + 1].rearrange("b (p j) n -> p b j n", j=PACK),
            )

        def add_up(b):
            for j in range(PACK):
                nc.tensor.matmul(
                    out=col_sum,
                    lhsT=raw[:, b, j, :],
                    rhs=ones_bf16[:, 0:1],
                    start=(b == SUMMED_B[0] and j == 0),
                    stop=(b == SUMMED_B[-1] and j == PACK - 1),
                )

        def regroup(b):
            if b not in ADDED_B:
                nc.gpsimd.tensor_scalar(
                    out=grouped[:, b],
                    in0=raw[:, b].rearrange("p j n -> p n j"),
                    scalar1=1.0,
                    scalar2=0.0,
                    op0=ALU.mult,
                    op1=ALU.add,
                )
            else:
                i = ADDED_B.index(b)
                nc.vector.tensor_scalar(
                    out=grouped[:, b].rearrange("p (c i) j -> p c j i", i=4),
                    in0=raw[:, b].rearrange("p j (c i) -> p c j i", i=4),
                    scalar1=1.0,
                    scalar2=None,
                    op0=ALU.mult,
                    op1=ALU.add,
                    accum_out=added[:, i : i + 1],
                )

        def flip(b):
            flipped = banks.tile([P, F], BF16, tag="bank", name="flipped")
            for j in range(PACK):
                nc.tensor.transpose(
                    flipped[:, j * P : (j + 1) * P], raw[:, b, j, :], ident_bf16[:]
                )
            return flipped

        for b in ADDED_B + (0, 1, 2, 3, 4, 8, 9):
            regroup(b)

        def repeat_rows(g):
            rows = banks.tile([P, BANK_COLS], F32, tag="bank", name="rows")
            for i in range(BANK_B):
                b = g * BANK_B + i
                nc.tensor.transpose(
                    rows[:, i * N : (i + 1) * N], sq_raw(b).to_broadcast([P, P]), ident[:]
                )
            return rows

        for b in ORDER:
            flipped = flip(b)
            if b in SCALAR_B:
                nc.scalar.activation(
                    out=squares[:, b, :],
                    in_=flipped[:],
                    func=ACT.Square,
                    accum_out=sq_raw(b),
                )
            else:
                nc.vector.bn_stats(
                    out=stats[:, 2 * b : 2 * b + 2].rearrange("p e s -> p (e s)"), in_=flipped[:]
                )

        for b in SUMMED_B:
            add_up(b)

        means = stats[:, 0:HALVES, 1]
        unread_sums = keep.tile([P, HALVES], F32)
        total_sum = keep.tile([P, 1], F32)
        point_sq = keep.tile([P, 1], F32)
        mean_term = keep.tile([P, 1], F32)
        nc.vector.tensor_scalar(
            out=unread_sums[:, 0 : len(ADDED_B)],
            in0=added[:],
            scalar1=1.0,
            scalar2=col_sum,
            op0=ALU.mult,
            op1=ALU.add,
            accum_out=stats[:, HALVES, 1:2],
        )
        nc.scalar.activation(
            out=stats[:, 0:HALVES, 0], in_=means, func=ACT.Square, scale=math.sqrt(F / 2.0)
        )
        nc.tensor.matmul(
            out=total_means, lhsT=ones_f32[:], rhs=stats[:, 0 : HALVES + 1, 1], start=True, stop=True
        )
        nc.vector.tensor_reduce(
            out=point_sq[:], in_=stats[:, :, 0:3:2], axis=mybir.AxisListType.XY, op=ALU.add
        )
        total_sq = banks.tile([P, 1], F32, tag="bank")
        nc.tensor.matmul(out=total_sq[:], lhsT=ones_f32[:], rhs=point_sq[:], start=True, stop=True)
        nc.vector.tensor_reduce(
            out=sq_vector[:],
            in_=stats[:, 0:HALVES, 0:3:2].rearrange("p (b e) s -> p b e s", e=2),
            axis=mybir.AxisListType.XY,
            op=ALU.add,
        )
        nc.vector.tensor_scalar(
            out=unread_sums[:],
            in0=total_means[:, 0:HALVES],
            scalar1=F / 2.0,
            scalar2=total_means[:, HALVES : HALVES + 1],
            op0=ALU.mult,
            op1=ALU.add,
            accum_out=total_sum[:],
        )

        rows = [repeat_rows(g) for g in range(GROUPS)]
        nc.scalar.activation(
            out=mean_term[:],
            in_=total_sum[:],
            func=ACT.Square,
            scale=1.0 / math.sqrt(COUNT * (COUNT - 1)),
        )

        rstd = keep.tile([P, 1], F32)
        nc.scalar.activation(
            out=rstd[:],
            in_=total_sq[:],
            func=ACT.Abs_reciprocal_sqrt,
            scale=-1.0 / (COUNT - 1),
            bias=mean_term[:],
        )

        def scale_on_vector(first, after):
            nc.vector.tensor_scalar(
                out=coord[:, first:after, :],
                in0=grouped[:, first:after].rearrange("p b n j -> p b (n j)"),
                scalar1=rstd[:],
                scalar2=None,
                op0=ALU.mult,
            )

        scale_on_vector(0, 4)
        scale_on_vector(4, 8)
        nc.scalar.activation(
            out=coord[:, GROUPED_B:].rearrange("p b (n j) -> p b n j", j=PACK),
            in_=raw[:, GROUPED_B:].rearrange("p b j n -> p b n j"),
            func=ACT.Copy,
            scale=rstd[:],
        )
        for b in range(B):
            i = b % BANK_B
            nc.scalar.activation(
                out=pair_raw[:, b, :],
                in_=rows[b // BANK_B][:, i * N : (i + 1) * N],
                func=ACT.Identity,
                bias=sq_raw(b),
            )
        nc.scalar.activation(out=unread[:, 1:2], in_=one[:], func=ACT.Exp)
        neg_half_rvar = keep.tile([P, 1], F32)
        nc.vector.scalar_tensor_tensor(
            out=neg_half_rvar[:], in0=rstd[:], scalar=-0.5, in1=rstd[:], op0=ALU.mult, op1=ALU.mult
        )

        def products(g):
            nc.vector.quantize_mx(
                out=codes[:, g, :].bitcast(FP8X4),
                scales=planes[:, g, :],
                in_=coord[:, group_batches(g)].rearrange("p b c -> p (b c)"),
            )
            inner = banks.tile([P, BANK_COLS], F32, tag="bank", name="inner")
            for i in range(BANK_B):
                cols = slice(i * N, (i + 1) * N)
                nc.tensor.matmul_mx(
                    out=inner[:, cols],
                    lhsT=codes[:, g, cols].bitcast(FP8X4),
                    lhsT_scale=planes[:, g, cols],
                    rhs=codes[:, g, cols].bitcast(FP8X4),
                    rhs_scale=planes[:, g, cols],
                    start=True,
                    stop=True,
                )
            return inner

        def subtract(first, after, inner):
            nc.vector.scalar_tensor_tensor(
                out=arg[:, first:after, :],
                in0=pair_raw[:, first:after, :],
                scalar=neg_half_rvar[:],
                in1=inner.rearrange("p (b m) -> p b m", m=N),
                op0=ALU.mult,
                op1=ALU.add,
            )

        def clamp(first, after):
            nc.vector.tensor_scalar_min(
                out=clamped[:, first:after, :], in0=arg[:, first:after, :], scalar1=0.0
            )

        def finish(first, after):
            nc.scalar.activation(
                out=result[:, first:after, :],
                in_=clamped[:, first:after, :],
                func=ACT.Exp,
                scale=1.0 / F,
            )
            nc.sync.dma_start(
                out=out[first:after].rearrange("b n m -> n b m"), in_=result[:, first:after, :]
            )

        inner0 = products(0)
        inner1 = products(1)
        scale_on_vector(8, GROUPED_B)
        subtract(0, 4, inner0[:])
        inner2 = products(2)
        clamp(0, 4)
        finish(0, 4)
        subtract(4, 8, inner1[:])
        subtract(8, 10, inner2[:, : 2 * N])
        clamp(4, 8)
        finish(4, 8)
        subtract(10, 12, inner2[:, 2 * N :])
        clamp(8, 10)
        finish(8, 10)
        clamp(10, 12)
        finish(10, 12)
